import numpy as np
import ml_dtypes


def mxq(x, axis, fmt="e4m3"):
    dtype, down = {"e4m3": (ml_dtypes.float8_e4m3fn, 7), "e5m2": (ml_dtypes.float8_e5m2, 14)}[fmt]
    v = np.moveaxis(np.asarray(x, np.float32).astype(ml_dtypes.bfloat16).astype(np.float64), axis, -1)
    blocks = v.reshape(v.shape[:-1] + (-1, 32))
    amax = np.abs(blocks).max(-1, keepdims=True)
    byte = np.maximum(np.where(amax > 0, np.frexp(amax)[1] - 1 + 127, 0) - down, 1)
    scale = np.exp2(byte - 127.0)
    codes = (blocks / scale).astype(np.float32).astype(dtype).astype(np.float64)
    return np.moveaxis((codes * scale).reshape(v.shape), -1, axis)


WIDE = False


def mx_kscale(k):
    if not WIDE:
        return np.ones(k)
    levels = np.array([10, -10, 5, -5, 0])
    a = np.random.permutation(np.resize(levels, k // 512 * 4)).reshape(k // 512, 4)
    idx = np.arange(k)
    return np.exp2(a[idx // 512, idx % 128 // 32])


BF16 = ml_dtypes.bfloat16


def bf(x):
    return np.asarray(x, np.float32).astype(BF16)


def f64(x):
    return np.asarray(x).astype(np.float64)


B, N = 512, 640
SLOPE = 0.01


def setup_inputs():
    s = mx_kscale(B)
    level = np.random.standard_normal(N) * 2.5 - 1.5
    return {"potential": bf((np.random.standard_normal((B, N)) * 2.2 + level) * s[:, None]),
            "contribution": bf(np.random.random(B) / (s * s))}


def reference(potential, contribution):
    p = f64(potential)
    activation = np.where(p >= 0, p, SLOPE * p)
    weighted = activation * f64(contribution)[:, None]
    return (mxq(weighted, 0, "e4m3").T @ mxq(activation, 0, "e4m3")) / B

@@ -1,0 +1,101 @@
+from contextlib import ExitStack
+
+import concourse.mybir as mybir
+
+F32 = mybir.dt.float32
+BF16 = mybir.dt.bfloat16
+U32 = mybir.dt.uint32
+U8 = mybir.dt.uint8
+FP8X4 = mybir.dt.float8_e4m3fn_x4
+ALU = mybir.AluOpType
+
+P = 128
+PACK = 4
+SAMPLES = P * PACK
+NEURONS = 640
+BLOCK = 128
+N_BLOCKS = NEURONS // BLOCK
+WIDE = 512
+SLOPE = 0.01
+
+FLOPS = 2 * SAMPLES * NEURONS * NEURONS
+
+
+def tile_mnelayer_pb_s_kernel(tc, potential, contribution, out):
+    nc = tc.nc
+    with ExitStack() as ctx:
+        keep = ctx.enter_context(tc.tile_pool(name="keep", bufs=1))
+        stored = ctx.enter_context(tc.tile_pool(name="stored", bufs=N_BLOCKS))
+        psum = ctx.enter_context(tc.psum_pool(name="psum", bufs=4))
+
+        pot = keep.tile([P, PACK, NEURONS], BF16)
+        contrib = keep.tile([P, PACK], BF16)
+        act_f32 = keep.tile([P, NEURONS, PACK], F32)
+        act_by_neuron = keep.tile([P, NEURONS, PACK], BF16, align_bytes=64)
+        wgt_by_neuron = keep.tile([P, NEURONS, PACK], BF16, align_bytes=64)
+        act_codes = keep.tile([P, NEURONS], U32, align_bytes=64)
+        act_scales = keep.tile([P, NEURONS], U8, align_bytes=64)
+        wgt_codes = keep.tile([P, NEURONS], U32, align_bytes=64)
+        wgt_scales = keep.tile([P, NEURONS], U8, align_bytes=64)
+
+        def block(b):
+            return slice(b * BLOCK, (b + 1) * BLOCK)
+
+        def quantise(values, codes, scales, neurons):
+            nc.vector.quantize_mx(
+                out=codes[:, neurons].bitcast(FP8X4),
+                scales=scales[:, neurons],
+                in_=values[:, neurons, :].rearrange("p w t -> p (w t)"),
+            )
+
+        def activate(b):
+            x = pot[:, :, block(b)].rearrange("p t w -> p w t")
+            nc.vector.scalar_tensor_tensor(
+                out=act_f32[:, block(b), :], in0=x, scalar=SLOPE, in1=x, op0=ALU.mult, op1=ALU.max
+            )
+            nc.scalar.copy(out=act_by_neuron[:, block(b), :], in_=act_f32[:, block(b), :])
+
+        def weigh(b):
+            nc.vector.tensor_tensor(
+                out=wgt_by_neuron[:, block(b), :],
+                in0=act_f32[:, block(b), :],
+                in1=contrib[:].unsqueeze(1).to_broadcast([P, BLOCK, PACK]),
+                op=ALU.mult,
+            )
+
+        def multiply(b, acc, neurons):
+            nc.tensor.matmul_mx(
+                out=acc[:],
+                lhsT=wgt_codes[:, block(b)].bitcast(FP8X4),
+                lhsT_scale=wgt_scales[:, block(b)],
+                rhs=act_codes[:, neurons].bitcast(FP8X4),
+                rhs_scale=act_scales[:, neurons],
+                start=True,
+                stop=True,
+            )
+
+        nc.scalar.dma_start(out=contrib[:], in_=contribution.rearrange("(p t) -> p t", t=PACK))
+        by_partition = potential.rearrange("(p t) w -> p t w", t=PACK)
+        for b in range(N_BLOCKS):
+            nc.sync.dma_start(out=pot[:, :, block(b)], in_=by_partition[:, :, block(b)])
+
+        for b in range(N_BLOCKS):
+            activate(b)
+
+        weigh(0)
+        quantise(act_by_neuron, act_codes, act_scales, slice(0, WIDE))
+        weigh(1)
+        quantise(act_by_neuron, act_codes, act_scales, slice(WIDE, NEURONS))
+
+        for b in range(N_BLOCKS):
+            quantise(wgt_by_neuron, wgt_codes, wgt_scales, block(b))
+            if b + 2 < N_BLOCKS:
+                weigh(b + 2)
+            wide = psum.tile([P, WIDE], F32)
+            narrow = psum.tile([P, NEURONS - WIDE], F32)
+            multiply(b, wide, slice(0, WIDE))
+            multiply(b, narrow, slice(WIDE, NEURONS))
+            rows = stored.tile([P, NEURONS], F32)
+            nc.scalar.mul(out=rows[:, 0:WIDE], in_=wide[:], mul=1.0 / SAMPLES)
+            nc.scalar.mul(out=rows[:, WIDE:NEURONS], in_=narrow[:], mul=1.0 / SAMPLES)
+            nc.sync.dma_start(out=out[block(b), :], in_=rows[:])

@@ -63,16 +63,35 @@ def tile_mnelayer_pb_s_kernel(tc, potential, contribution, out):
                 op=ALU.mult,
             )
 
-        def multiply(b, acc, neurons):
-            nc.tensor.matmul_mx(
-                out=acc[:],
-                lhsT=wgt_codes[:, block(b)].bitcast(FP8X4),
-                lhsT_scale=wgt_scales[:, block(b)],
-                rhs=act_codes[:, neurons].bitcast(FP8X4),
-                rhs_scale=act_scales[:, neurons],
-                start=True,
-                stop=True,
-            )
+        def multiply(b):
+            wide = psum.tile([P, WIDE], F32)
+            narrow = psum.tile([P, NEURONS - WIDE], F32)
+            for acc, neurons in ((wide, slice(0, WIDE)), (narrow, slice(WIDE, NEURONS))):
+                nc.tensor.matmul_mx(
+                    out=acc[:],
+                    lhsT=wgt_codes[:, block(b)].bitcast(FP8X4),
+                    lhsT_scale=wgt_scales[:, block(b)],
+                    rhs=act_codes[:, neurons].bitcast(FP8X4),
+                    rhs_scale=act_scales[:, neurons],
+                    start=True,
+                    stop=True,
+                )
+            return wide, narrow
+
+        def scale_on_scalar(dst, src):
+            nc.scalar.mul(out=dst, in_=src, mul=1.0 / SAMPLES)
+
+        def scale_on_vector(dst, src):
+            nc.vector.tensor_scalar_mul(out=dst, in0=src, scalar1=1.0 / SAMPLES)
+
+        def store(b, banks, scale):
+            wide, narrow = banks
+            rows = stored.tile([P, NEURONS], F32)
+            scale(rows[:, 0:WIDE], wide[:])
+            scale(rows[:, WIDE:NEURONS], narrow[:])
+            nc.sync.dma_start(out=out[block(b), :], in_=rows[:])
+
+        ctx.enter_context(tc.manual_schedule())
 
         nc.scalar.dma_start(out=contrib[:], in_=contribution.rearrange("(p t) -> p t", t=PACK))
         by_partition = potential.rearrange("(p t) w -> p t w", t=PACK)
@@ -87,15 +106,13 @@ def tile_mnelayer_pb_s_kernel(tc, potential, contribution, out):
         weigh(1)
         quantise(act_by_neuron, act_codes, act_scales, slice(WIDE, NEURONS))
 
+        banks = []
         for b in range(N_BLOCKS):
             quantise(wgt_by_neuron, wgt_codes, wgt_scales, block(b))
             if b + 2 < N_BLOCKS:
                 weigh(b + 2)
-            wide = psum.tile([P, WIDE], F32)
-            narrow = psum.tile([P, NEURONS - WIDE], F32)
-            multiply(b, wide, slice(0, WIDE))
-            multiply(b, narrow, slice(WIDE, NEURONS))
-            rows = stored.tile([P, NEURONS], F32)
-            nc.scalar.mul(out=rows[:, 0:WIDE], in_=wide[:], mul=1.0 / SAMPLES)
-            nc.scalar.mul(out=rows[:, WIDE:NEURONS], in_=narrow[:], mul=1.0 / SAMPLES)
-            nc.sync.dma_start(out=out[block(b), :], in_=rows[:])
+            banks.append(multiply(b))
+            if b < N_BLOCKS - 2:
+                store(b, banks[b], scale_on_scalar)
+        store(N_BLOCKS - 2, banks[N_BLOCKS - 2], scale_on_vector)
+        store(N_BLOCKS - 1, banks[N_BLOCKS - 1], scale_on_scalar)

@@ -15,7 +15,8 @@ SAMPLES = P * PACK
 NEURONS = 640
 BLOCK = 128
 N_BLOCKS = NEURONS // BLOCK
-WIDE = 512
+WIDE = (0, 512)
+NARROW = (512, 128)
 SLOPE = 0.01
 
 FLOPS = 2 * SAMPLES * NEURONS * NEURONS
@@ -25,8 +26,8 @@ def tile_mnelayer_pb_s_kernel(tc, potential, contribution, out):
     nc = tc.nc
     with ExitStack() as ctx:
         keep = ctx.enter_context(tc.tile_pool(name="keep", bufs=1))
-        stored = ctx.enter_context(tc.tile_pool(name="stored", bufs=N_BLOCKS))
-        psum = ctx.enter_context(tc.psum_pool(name="psum", bufs=4))
+        stored = ctx.enter_context(tc.tile_pool(name="stored", bufs=2 * N_BLOCKS))
+        psum = ctx.enter_context(tc.psum_pool(name="psum", bufs=7))
 
         pot = keep.tile([P, PACK, NEURONS], BF16)
         contrib = keep.tile([P, PACK], BF16)
@@ -40,6 +41,9 @@ def tile_mnelayer_pb_s_kernel(tc, potential, contribution, out):
 
         def block(b):
             return slice(b * BLOCK, (b + 1) * BLOCK)
+
+        def columns(part):
+            return slice(part[0], part[0] + part[1])
 
         def quantise(values, codes, scales, neurons):
             nc.vector.quantize_mx(
@@ -63,20 +67,18 @@ def tile_mnelayer_pb_s_kernel(tc, potential, contribution, out):
                 op=ALU.mult,
             )
 
-        def multiply(b):
-            wide = psum.tile([P, WIDE], F32)
-            narrow = psum.tile([P, NEURONS - WIDE], F32)
-            for acc, neurons in ((wide, slice(0, WIDE)), (narrow, slice(WIDE, NEURONS))):
-                nc.tensor.matmul_mx(
-                    out=acc[:],
-                    lhsT=wgt_codes[:, block(b)].bitcast(FP8X4),
-                    lhsT_scale=wgt_scales[:, block(b)],
-                    rhs=act_codes[:, neurons].bitcast(FP8X4),
-                    rhs_scale=act_scales[:, neurons],
-                    start=True,
-                    stop=True,
-                )
-            return wide, narrow
+        def multiply(b, part):
+            bank = psum.tile([P, part[1]], F32)
+            nc.tensor.matmul_mx(
+                out=bank[:],
+                lhsT=wgt_codes[:, block(b)].bitcast(FP8X4),
+                lhsT_scale=wgt_scales[:, block(b)],
+                rhs=act_codes[:, columns(part)].bitcast(FP8X4),
+                rhs_scale=act_scales[:, columns(part)],
+                start=True,
+                stop=True,
+            )
+            return bank
 
         def scale_on_scalar(dst, src):
             nc.scalar.mul(out=dst, in_=src, mul=1.0 / SAMPLES)
@@ -84,12 +86,10 @@ def tile_mnelayer_pb_s_kernel(tc, potential, contribution, out):
         def scale_on_vector(dst, src):
             nc.vector.tensor_scalar_mul(out=dst, in0=src, scalar1=1.0 / SAMPLES)
 
-        def store(b, banks, scale):
-            wide, narrow = banks
-            rows = stored.tile([P, NEURONS], F32)
-            scale(rows[:, 0:WIDE], wide[:])
-            scale(rows[:, WIDE:NEURONS], narrow[:])
-            nc.sync.dma_start(out=out[block(b), :], in_=rows[:])
+        def store(b, part, bank, scale):
+            piece = stored.tile([P, part[1]], F32)
+            scale(piece[:], bank[:])
+            nc.sync.dma_start(out=out[block(b), columns(part)], in_=piece[:])
 
         ctx.enter_context(tc.manual_schedule())
 
@@ -102,17 +102,20 @@ def tile_mnelayer_pb_s_kernel(tc, potential, contribution, out):
             activate(b)
 
         weigh(0)
-        quantise(act_by_neuron, act_codes, act_scales, slice(0, WIDE))
+        quantise(act_by_neuron, act_codes, act_scales, columns(WIDE))
         weigh(1)
-        quantise(act_by_neuron, act_codes, act_scales, slice(WIDE, NEURONS))
+        quantise(act_by_neuron, act_codes, act_scales, columns(NARROW))
 
         banks = []
         for b in range(N_BLOCKS):
             quantise(wgt_by_neuron, wgt_codes, wgt_scales, block(b))
             if b + 2 < N_BLOCKS:
                 weigh(b + 2)
-            banks.append(multiply(b))
+            banks.append((multiply(b, WIDE), multiply(b, NARROW)))
             if b < N_BLOCKS - 2:
-                store(b, banks[b], scale_on_scalar)
-        store(N_BLOCKS - 2, banks[N_BLOCKS - 2], scale_on_vector)
-        store(N_BLOCKS - 1, banks[N_BLOCKS - 1], scale_on_scalar)
+                store(b, WIDE, banks[b][0], scale_on_scalar)
+                store(b, NARROW, banks[b][1], scale_on_scalar)
+        store(N_BLOCKS - 2, WIDE, banks[N_BLOCKS - 2][0], scale_on_vector)
+        store(N_BLOCKS - 1, WIDE, banks[N_BLOCKS - 1][0], scale_on_scalar)
+        store(N_BLOCKS - 2, NARROW, banks[N_BLOCKS - 2][1], scale_on_vector)
+        store(N_BLOCKS - 1, NARROW, banks[N_BLOCKS - 1][1], scale_on_vector)

@@ -6,6 +6,7 @@ F32 = mybir.dt.float32
 BF16 = mybir.dt.bfloat16
 U32 = mybir.dt.uint32
 U8 = mybir.dt.uint8
+I32 = mybir.dt.int32
 FP8X4 = mybir.dt.float8_e4m3fn_x4
 ALU = mybir.AluOpType
 
@@ -18,6 +19,7 @@ N_BLOCKS = NEURONS // BLOCK
 WIDE = (0, 512)
 NARROW = (512, 128)
 SLOPE = 0.01
+WARM_PASSES = 15
 
 FLOPS = 2 * SAMPLES * NEURONS * NEURONS
 
@@ -28,6 +30,7 @@ def tile_mnelayer_pb_s_kernel(tc, potential, contribution, out):
         keep = ctx.enter_context(tc.tile_pool(name="keep", bufs=1))
         stored = ctx.enter_context(tc.tile_pool(name="stored", bufs=2 * N_BLOCKS))
         psum = ctx.enter_context(tc.psum_pool(name="psum", bufs=7))
+        idle = ctx.enter_context(tc.psum_pool(name="idle", bufs=1))
 
         pot = keep.tile([P, PACK, NEURONS], BF16)
         contrib = keep.tile([P, PACK], BF16)
@@ -97,6 +100,23 @@ def tile_mnelayer_pb_s_kernel(tc, potential, contribution, out):
         by_partition = potential.rearrange("(p t) w -> p t w", t=PACK)
         for b in range(N_BLOCKS):
             nc.sync.dma_start(out=pot[:, :, block(b)], in_=by_partition[:, :, block(b)])
+
+        zeros = keep.tile([P, PACK * WIDE[1]], BF16, align_bytes=64)
+        zero_codes = keep.tile([P, WIDE[1]], U32, align_bytes=64)
+        zero_scales = keep.tile([P, WIDE[1]], U8, align_bytes=64)
+        nc.vector.memset(zeros[:].bitcast(I32), 0)
+        nc.vector.quantize_mx(out=zero_codes[:].bitcast(FP8X4), scales=zero_scales[:], in_=zeros[:])
+        unread = idle.tile([P, WIDE[1]], F32)
+        for i in range(WARM_PASSES):
+            nc.tensor.matmul_mx(
+                out=unread[:],
+                lhsT=zero_codes[:, 0:BLOCK].bitcast(FP8X4),
+                lhsT_scale=zero_scales[:, 0:BLOCK],
+                rhs=zero_codes[:].bitcast(FP8X4),
+                rhs_scale=zero_scales[:],
+                start=True,
+                stop=True,
+            )
 
         for b in range(N_BLOCKS):
             activate(b)

@@ -19,7 +19,7 @@ N_BLOCKS = NEURONS // BLOCK
 WIDE = (0, 512)
 NARROW = (512, 128)
 SLOPE = 0.01
-WARM_PASSES = 15
+WARM_PASSES = 12
 
 FLOPS = 2 * SAMPLES * NEURONS * NEURONS
 
@@ -28,7 +28,7 @@ def tile_mnelayer_pb_s_kernel(tc, potential, contribution, out):
     nc = tc.nc
     with ExitStack() as ctx:
         keep = ctx.enter_context(tc.tile_pool(name="keep", bufs=1))
-        stored = ctx.enter_context(tc.tile_pool(name="stored", bufs=2 * N_BLOCKS))
+        stored = ctx.enter_context(tc.tile_pool(name="stored", bufs=2 * N_BLOCKS + 1))
         psum = ctx.enter_context(tc.psum_pool(name="psum", bufs=7))
         idle = ctx.enter_context(tc.psum_pool(name="idle", bufs=1))
 
@@ -62,11 +62,11 @@ def tile_mnelayer_pb_s_kernel(tc, potential, contribution, out):
             )
             nc.scalar.copy(out=act_by_neuron[:, block(b), :], in_=act_f32[:, block(b), :])
 
-        def weigh(b):
+        def weigh(neurons):
             nc.vector.tensor_tensor(
-                out=wgt_by_neuron[:, block(b), :],
-                in0=act_f32[:, block(b), :],
-                in1=contrib[:].unsqueeze(1).to_broadcast([P, BLOCK, PACK]),
+                out=wgt_by_neuron[:, neurons, :],
+                in0=act_f32[:, neurons, :],
+                in1=contrib[:].unsqueeze(1).to_broadcast([P, neurons.stop - neurons.start, PACK]),
                 op=ALU.mult,
             )
 
@@ -118,24 +118,34 @@ def tile_mnelayer_pb_s_kernel(tc, potential, contribution, out):
                 stop=True,
             )
 
-        for b in range(N_BLOCKS):
+        def product(b, part, scale):
+            store(b, part, multiply(b, part), scale)
+
+        for b in range(4):
             activate(b)
-
-        weigh(0)
+        weigh(block(0))
+        weigh(block(1))
         quantise(act_by_neuron, act_codes, act_scales, columns(WIDE))
-        weigh(1)
+        quantise(wgt_by_neuron, wgt_codes, wgt_scales, block(0))
+        product(0, WIDE, scale_on_scalar)
+        quantise(wgt_by_neuron, wgt_codes, wgt_scales, block(1))
+        product(1, WIDE, scale_on_scalar)
+        weigh(block(2))
+        activate(4)
+        quantise(wgt_by_neuron, wgt_codes, wgt_scales, block(2))
+        product(2, WIDE, scale_on_scalar)
+        weigh(block(3))
         quantise(act_by_neuron, act_codes, act_scales, columns(NARROW))
-
-        banks = []
-        for b in range(N_BLOCKS):
-            quantise(wgt_by_neuron, wgt_codes, wgt_scales, block(b))
-            if b + 2 < N_BLOCKS:
-                weigh(b + 2)
-            banks.append((multiply(b, WIDE), multiply(b, NARROW)))
-            if b < N_BLOCKS - 2:
-                store(b, WIDE, banks[b][0], scale_on_scalar)
-                store(b, NARROW, banks[b][1], scale_on_scalar)
-        store(N_BLOCKS - 2, WIDE, banks[N_BLOCKS - 2][0], scale_on_vector)
-        store(N_BLOCKS - 1, WIDE, banks[N_BLOCKS - 1][0], scale_on_scalar)
-        store(N_BLOCKS - 2, NARROW, banks[N_BLOCKS - 2][1], scale_on_vector)
-        store(N_BLOCKS - 1, NARROW, banks[N_BLOCKS - 1][1], scale_on_vector)
+        for b in range(2):
+            product(b, NARROW, scale_on_scalar)
+        narrow_2 = multiply(2, NARROW)
+        quantise(wgt_by_neuron, wgt_codes, wgt_scales, block(3))
+        product(3, WIDE, scale_on_scalar)
+        product(3, NARROW, scale_on_scalar)
+        weigh(block(4))
+        store(2, NARROW, narrow_2, scale_on_vector)
+        quantise(wgt_by_neuron, wgt_codes, wgt_scales, block(4))
+        last = [multiply(4, part) for part in ((0, 256), (256, 256), (512, 128))]
+        store(4, (0, 256), last[0], scale_on_vector)
+        store(4, (256, 256), last[1], scale_on_scalar)
+        store(4, (512, 128), last[2], scale_on_vector)

@@ -1,6 +1,7 @@
 from contextlib import ExitStack
 
 import concourse.mybir as mybir
+from concourse.masks import make_identity
 
 F32 = mybir.dt.float32
 BF16 = mybir.dt.bfloat16
@@ -19,7 +20,9 @@ N_BLOCKS = NEURONS // BLOCK
 WIDE = (0, 512)
 NARROW = (512, 128)
 SLOPE = 0.01
-WARM_PASSES = 12
+ON_TENSOR = 2
+WARM_PASSES = 16
+FILL_PASSES = 14
 
 FLOPS = 2 * SAMPLES * NEURONS * NEURONS
 
@@ -28,12 +31,16 @@ def tile_mnelayer_pb_s_kernel(tc, potential, contribution, out):
     nc = tc.nc
     with ExitStack() as ctx:
         keep = ctx.enter_context(tc.tile_pool(name="keep", bufs=1))
-        stored = ctx.enter_context(tc.tile_pool(name="stored", bufs=2 * N_BLOCKS + 1))
-        psum = ctx.enter_context(tc.psum_pool(name="psum", bufs=7))
+        stored = ctx.enter_context(tc.tile_pool(name="stored", bufs=10))
+        psum = ctx.enter_context(tc.psum_pool(name="psum", bufs=5))
+        weighed = ctx.enter_context(tc.psum_pool(name="weighed", bufs=ON_TENSOR))
         idle = ctx.enter_context(tc.psum_pool(name="idle", bufs=1))
 
         pot = keep.tile([P, PACK, NEURONS], BF16)
         contrib = keep.tile([P, PACK], BF16)
+        ident = keep.tile([P, P], F32)
+        diag = keep.tile([P, PACK, P], F32)
+        act_rows = keep.tile([P, PACK, ON_TENSOR * BLOCK], F32)
         act_f32 = keep.tile([P, NEURONS, PACK], F32)
         act_by_neuron = keep.tile([P, NEURONS, PACK], BF16, align_bytes=64)
         wgt_by_neuron = keep.tile([P, NEURONS, PACK], BF16, align_bytes=64)
@@ -55,25 +62,54 @@ def tile_mnelayer_pb_s_kernel(tc, potential, contribution, out):
                 in_=values[:, neurons, :].rearrange("p w t -> p (w t)"),
             )
 
-        def activate(b):
+        def quantise_act(part):
+            quantise(act_by_neuron, act_codes, act_scales, columns(part))
+
+        def quantise_wgt(b):
+            quantise(wgt_by_neuron, wgt_codes, wgt_scales, block(b))
+
+        def leaky(b):
             x = pot[:, :, block(b)].rearrange("p t w -> p w t")
             nc.vector.scalar_tensor_tensor(
                 out=act_f32[:, block(b), :], in0=x, scalar=SLOPE, in1=x, op0=ALU.mult, op1=ALU.max
             )
+
+        def activate(b):
+            leaky(b)
             nc.scalar.copy(out=act_by_neuron[:, block(b), :], in_=act_f32[:, block(b), :])
 
-        def weigh(neurons):
+        def activate_rows(b):
+            x = pot[:, :, block(b)]
+            nc.vector.scalar_tensor_tensor(
+                out=act_rows[:, :, block(b)], in0=x, scalar=SLOPE, in1=x, op0=ALU.mult, op1=ALU.max
+            )
+            nc.scalar.copy(
+                out=act_by_neuron[:, block(b), :],
+                in_=act_rows[:, :, block(b)].rearrange("p t w -> p w t"),
+            )
+
+        def weigh(b):
             nc.vector.tensor_tensor(
-                out=wgt_by_neuron[:, neurons, :],
-                in0=act_f32[:, neurons, :],
-                in1=contrib[:].unsqueeze(1).to_broadcast([P, neurons.stop - neurons.start, PACK]),
+                out=wgt_by_neuron[:, block(b), :],
+                in0=act_f32[:, block(b), :],
+                in1=contrib[:].unsqueeze(1).to_broadcast([P, BLOCK, PACK]),
                 op=ALU.mult,
             )
 
-        def multiply(b, part):
-            bank = psum.tile([P, part[1]], F32)
+        def weigh_on_tensor(b):
+            bank = weighed.tile([P, PACK, BLOCK], F32)
+            for t in range(PACK):
+                nc.tensor.matmul(
+                    out=bank[:, t, :], lhsT=diag[:, t, :], rhs=act_rows[:, t, block(b)], start=True, stop=True
+                )
+            return bank
+
+        def round_weighed(b, bank):
+            nc.scalar.copy(out=wgt_by_neuron[:, block(b), :], in_=bank[:].rearrange("p t w -> p w t"))
+
+        def pass_mx(dst, b, part):
             nc.tensor.matmul_mx(
-                out=bank[:],
+                out=dst,
                 lhsT=wgt_codes[:, block(b)].bitcast(FP8X4),
                 lhsT_scale=wgt_scales[:, block(b)],
                 rhs=act_codes[:, columns(part)].bitcast(FP8X4),
@@ -81,6 +117,16 @@ def tile_mnelayer_pb_s_kernel(tc, potential, contribution, out):
                 start=True,
                 stop=True,
             )
+
+        def multiply(b, part):
+            bank = psum.tile([P, part[1]], F32)
+            pass_mx(bank[:], b, part)
+            return bank
+
+        def multiply_narrow(first):
+            bank = psum.tile([P, 2, BLOCK], F32)
+            for i in range(2):
+                pass_mx(bank[:, i, :], first + i, NARROW)
             return bank
 
         def scale_on_scalar(dst, src):
@@ -94,58 +140,82 @@ def tile_mnelayer_pb_s_kernel(tc, potential, contribution, out):
             scale(piece[:], bank[:])
             nc.sync.dma_start(out=out[block(b), columns(part)], in_=piece[:])
 
-        ctx.enter_context(tc.manual_schedule())
-
-        nc.scalar.dma_start(out=contrib[:], in_=contribution.rearrange("(p t) -> p t", t=PACK))
-        by_partition = potential.rearrange("(p t) w -> p t w", t=PACK)
-        for b in range(N_BLOCKS):
-            nc.sync.dma_start(out=pot[:, :, block(b)], in_=by_partition[:, :, block(b)])
-
-        zeros = keep.tile([P, PACK * WIDE[1]], BF16, align_bytes=64)
-        zero_codes = keep.tile([P, WIDE[1]], U32, align_bytes=64)
-        zero_scales = keep.tile([P, WIDE[1]], U8, align_bytes=64)
-        nc.vector.memset(zeros[:].bitcast(I32), 0)
-        nc.vector.quantize_mx(out=zero_codes[:].bitcast(FP8X4), scales=zero_scales[:], in_=zeros[:])
-        unread = idle.tile([P, WIDE[1]], F32)
-        for i in range(WARM_PASSES):
-            nc.tensor.matmul_mx(
-                out=unread[:],
-                lhsT=zero_codes[:, 0:BLOCK].bitcast(FP8X4),
-                lhsT_scale=zero_scales[:, 0:BLOCK],
-                rhs=zero_codes[:].bitcast(FP8X4),
-                rhs_scale=zero_scales[:],
-                start=True,
-                stop=True,
-            )
+        def store_narrow(first, bank, scale):
+            piece = stored.tile([P, 2, BLOCK], F32)
+            scale(piece[:], bank[:])
+            rows = out[first * BLOCK : (first + 2) * BLOCK, columns(NARROW)]
+            nc.sync.dma_start(out=rows.rearrange("(i p) c -> p i c", p=P), in_=piece[:])
 
         def product(b, part, scale):
             store(b, part, multiply(b, part), scale)
 
-        for b in range(4):
-            activate(b)
-        weigh(block(0))
-        weigh(block(1))
-        quantise(act_by_neuron, act_codes, act_scales, columns(WIDE))
-        quantise(wgt_by_neuron, wgt_codes, wgt_scales, block(0))
-        product(0, WIDE, scale_on_scalar)
-        quantise(wgt_by_neuron, wgt_codes, wgt_scales, block(1))
-        product(1, WIDE, scale_on_scalar)
-        weigh(block(2))
-        activate(4)
-        quantise(wgt_by_neuron, wgt_codes, wgt_scales, block(2))
+        ctx.enter_context(tc.manual_schedule())
+
+        nc.sync.dma_start(out=contrib[:], in_=contribution.rearrange("(p t) -> p t", t=PACK))
+        by_partition = potential.rearrange("(p t) w -> p t w", t=PACK)
+        for b in range(N_BLOCKS):
+            nc.sync.dma_start(out=pot[:, :, block(b)], in_=by_partition[:, :, block(b)])
+
+        make_identity(nc, ident[:])
+
+        zeros = keep.tile([P, PACK * BLOCK], BF16, align_bytes=64)
+        zero_codes = keep.tile([P, BLOCK], U32, align_bytes=64)
+        zero_scales = keep.tile([P, BLOCK], U8, align_bytes=64)
+        nc.vector.memset(zeros[:].bitcast(I32), 0)
+        nc.vector.quantize_mx(out=zero_codes[:].bitcast(FP8X4), scales=zero_scales[:], in_=zeros[:])
+        unread = idle.tile([P, BLOCK], F32)
+
+        def idle_passes(count):
+            for i in range(count):
+                nc.tensor.matmul_mx(
+                    out=unread[:],
+                    lhsT=zero_codes[:].bitcast(FP8X4),
+                    lhsT_scale=zero_scales[:],
+                    rhs=zero_codes[:].bitcast(FP8X4),
+                    rhs_scale=zero_scales[:],
+                    start=True,
+                    stop=True,
+                )
+
+        idle_passes(WARM_PASSES)
+
+        nc.vector.tensor_tensor(
+            out=diag[:],
+            in0=ident[:].unsqueeze(1).to_broadcast([P, PACK, P]),
+            in1=contrib[:].unsqueeze(2).to_broadcast([P, PACK, P]),
+            op=ALU.mult,
+        )
+
+        banks = []
+        for b in range(ON_TENSOR):
+            activate_rows(b)
+            banks.append(weigh_on_tensor(b))
+        idle_passes(FILL_PASSES)
+        activate(2)
+        activate(3)
+        weigh(2)
+        quantise_wgt(2)
+        for b in range(ON_TENSOR):
+            round_weighed(b, banks[b])
+        quantise_act(WIDE)
         product(2, WIDE, scale_on_scalar)
-        weigh(block(3))
-        quantise(act_by_neuron, act_codes, act_scales, columns(NARROW))
-        for b in range(2):
-            product(b, NARROW, scale_on_scalar)
-        narrow_2 = multiply(2, NARROW)
-        quantise(wgt_by_neuron, wgt_codes, wgt_scales, block(3))
+        quantise_wgt(0)
+        product(0, WIDE, scale_on_scalar)
+        leaky(4)
+        quantise_wgt(1)
+        product(1, WIDE, scale_on_scalar)
+        weigh(3)
+        nc.vector.tensor_copy(out=act_by_neuron[:, block(4), :], in_=act_f32[:, block(4), :])
+        quantise_wgt(3)
         product(3, WIDE, scale_on_scalar)
-        product(3, NARROW, scale_on_scalar)
-        weigh(block(4))
-        store(2, NARROW, narrow_2, scale_on_vector)
-        quantise(wgt_by_neuron, wgt_codes, wgt_scales, block(4))
+        weigh(4)
+        quantise_act(NARROW)
+        narrow_01 = multiply_narrow(0)
+        narrow_23 = multiply_narrow(2)
+        quantise_wgt(4)
         last = [multiply(4, part) for part in ((0, 256), (256, 256), (512, 128))]
+        store_narrow(0, narrow_01, scale_on_vector)
+        store_narrow(2, narrow_23, scale_on_scalar)
         store(4, (0, 256), last[0], scale_on_vector)
         store(4, (256, 256), last[1], scale_on_scalar)
         store(4, (512, 128), last[2], scale_on_vector)

@@ -22,7 +22,7 @@ NARROW = (512, 128)
 SLOPE = 0.01
 ON_TENSOR = 2
 WARM_PASSES = 16
-FILL_PASSES = 14
+FILL_PASSES = 6
 
 FLOPS = 2 * SAMPLES * NEURONS * NEURONS
 
@@ -201,13 +201,13 @@ def tile_mnelayer_pb_s_kernel(tc, potential, contribution, out):
         product(2, WIDE, scale_on_scalar)
         quantise_wgt(0)
         product(0, WIDE, scale_on_scalar)
-        leaky(4)
+        weigh(3)
         quantise_wgt(1)
         product(1, WIDE, scale_on_scalar)
-        weigh(3)
-        nc.vector.tensor_copy(out=act_by_neuron[:, block(4), :], in_=act_f32[:, block(4), :])
+        leaky(4)
         quantise_wgt(3)
         product(3, WIDE, scale_on_scalar)
+        nc.vector.tensor_copy(out=act_by_neuron[:, block(4), :], in_=act_f32[:, block(4), :])
         weigh(4)
         quantise_act(NARROW)
         narrow_01 = multiply_narrow(0)

@@ -197,7 +197,8 @@ def tile_mnelayer_pb_s_kernel(tc, potential, contribution, out):
         quantise_wgt(2)
         for b in range(ON_TENSOR):
             round_weighed(b, banks[b])
-        quantise_act(WIDE)
+        quantise_act((0, 256))
+        quantise_act((256, 256))
         product(2, WIDE, scale_on_scalar)
         quantise_wgt(0)
         product(0, WIDE, scale_on_scalar)

@@ -20,6 +20,7 @@ N_BLOCKS = NEURONS // BLOCK
 WIDE = (0, 512)
 NARROW = (512, 128)
 SLOPE = 0.01
+SAMPLE_PAIRS = (slice(0, 2), slice(2, 4))
 ON_TENSOR = 2
 WARM_PASSES = 16
 FILL_PASSES = 6
@@ -38,6 +39,7 @@ def tile_mnelayer_pb_s_kernel(tc, potential, contribution, out):
 
         pot = keep.tile([P, PACK, NEURONS], BF16)
         contrib = keep.tile([P, PACK], BF16)
+        contrib_f32 = keep.tile([P, PACK], F32)
         ident = keep.tile([P, P], F32)
         diag = keep.tile([P, PACK, P], F32)
         act_rows = keep.tile([P, PACK, ON_TENSOR * BLOCK], F32)
@@ -79,10 +81,11 @@ def tile_mnelayer_pb_s_kernel(tc, potential, contribution, out):
             nc.scalar.copy(out=act_by_neuron[:, block(b), :], in_=act_f32[:, block(b), :])
 
         def activate_rows(b):
-            x = pot[:, :, block(b)]
-            nc.vector.scalar_tensor_tensor(
-                out=act_rows[:, :, block(b)], in0=x, scalar=SLOPE, in1=x, op0=ALU.mult, op1=ALU.max
-            )
+            for pair in SAMPLE_PAIRS:
+                x = pot[:, pair, block(b)]
+                nc.vector.scalar_tensor_tensor(
+                    out=act_rows[:, pair, block(b)], in0=x, scalar=SLOPE, in1=x, op0=ALU.mult, op1=ALU.max
+                )
             nc.scalar.copy(
                 out=act_by_neuron[:, block(b), :],
                 in_=act_rows[:, :, block(b)].rearrange("p t w -> p w t"),
@@ -151,10 +154,16 @@ def tile_mnelayer_pb_s_kernel(tc, potential, contribution, out):
 
         ctx.enter_context(tc.manual_schedule())
 
-        nc.sync.dma_start(out=contrib[:], in_=contribution.rearrange("(p t) -> p t", t=PACK))
+        nc.scalar.dma_start(out=contrib[:], in_=contribution.rearrange("(p t) -> p t", t=PACK))
         by_partition = potential.rearrange("(p t) w -> p t w", t=PACK)
-        for b in range(N_BLOCKS):
-            nc.sync.dma_start(out=pot[:, :, block(b)], in_=by_partition[:, :, block(b)])
+
+        def load(samples, neurons):
+            nc.sync.dma_start(out=pot[:, samples, neurons], in_=by_partition[:, samples, neurons])
+
+        for pair in SAMPLE_PAIRS:
+            load(pair, slice(0, 256))
+        load(slice(0, PACK), slice(256, 512))
+        load(slice(0, PACK), slice(512, 640))
 
         make_identity(nc, ident[:])
 
@@ -179,12 +188,14 @@ def tile_mnelayer_pb_s_kernel(tc, potential, contribution, out):
 
         idle_passes(WARM_PASSES)
 
-        nc.vector.tensor_tensor(
-            out=diag[:],
-            in0=ident[:].unsqueeze(1).to_broadcast([P, PACK, P]),
-            in1=contrib[:].unsqueeze(2).to_broadcast([P, PACK, P]),
-            op=ALU.mult,
-        )
+        nc.scalar.copy(out=contrib_f32[:], in_=contrib[:])
+        for t in range(PACK):
+            nc.scalar.activation(
+                out=diag[:, t, :],
+                in_=ident[:],
+                func=mybir.ActivationFunctionType.Copy,
+                scale=contrib_f32[:, t : t + 1],
+            )
 
         banks = []
         for b in range(ON_TENSOR):

@@ -17,13 +17,12 @@ SAMPLES = P * PACK
 NEURONS = 640
 BLOCK = 128
 N_BLOCKS = NEURONS // BLOCK
-WIDE = (0, 512)
+HALVES = ((0, 256), (256, 256))
 NARROW = (512, 128)
 SLOPE = 0.01
 SAMPLE_PAIRS = (slice(0, 2), slice(2, 4))
 ON_TENSOR = 2
 WARM_PASSES = 16
-FILL_PASSES = 6
 
 FLOPS = 2 * SAMPLES * NEURONS * NEURONS
 
@@ -32,9 +31,8 @@ def tile_mnelayer_pb_s_kernel(tc, potential, contribution, out):
     nc = tc.nc
     with ExitStack() as ctx:
         keep = ctx.enter_context(tc.tile_pool(name="keep", bufs=1))
-        stored = ctx.enter_context(tc.tile_pool(name="stored", bufs=10))
-        psum = ctx.enter_context(tc.psum_pool(name="psum", bufs=5))
-        weighed = ctx.enter_context(tc.psum_pool(name="weighed", bufs=ON_TENSOR))
+        stored = ctx.enter_context(tc.tile_pool(name="stored", bufs=14))
+        psum = ctx.enter_context(tc.psum_pool(name="psum", bufs=7))
         idle = ctx.enter_context(tc.psum_pool(name="idle", bufs=1))
 
         pot = keep.tile([P, PACK, NEURONS], BF16)
@@ -76,8 +74,7 @@ def tile_mnelayer_pb_s_kernel(tc, potential, contribution, out):
                 out=act_f32[:, block(b), :], in0=x, scalar=SLOPE, in1=x, op0=ALU.mult, op1=ALU.max
             )
 
-        def activate(b):
-            leaky(b)
+        def cast(b):
             nc.scalar.copy(out=act_by_neuron[:, block(b), :], in_=act_f32[:, block(b), :])
 
         def activate_rows(b):
@@ -100,7 +97,7 @@ def tile_mnelayer_pb_s_kernel(tc, potential, contribution, out):
             )
 
         def weigh_on_tensor(b):
-            bank = weighed.tile([P, PACK, BLOCK], F32)
+            bank = psum.tile([P, PACK, BLOCK], F32)
             for t in range(PACK):
                 nc.tensor.matmul(
                     out=bank[:, t, :], lhsT=diag[:, t, :], rhs=act_rows[:, t, block(b)], start=True, stop=True
@@ -201,33 +198,34 @@ def tile_mnelayer_pb_s_kernel(tc, potential, contribution, out):
         for b in range(ON_TENSOR):
             activate_rows(b)
             banks.append(weigh_on_tensor(b))
-        idle_passes(FILL_PASSES)
-        activate(2)
-        activate(3)
-        weigh(2)
-        quantise_wgt(2)
+        for b in (2, 3):
+            leaky(b)
+            cast(b)
         for b in range(ON_TENSOR):
             round_weighed(b, banks[b])
-        quantise_act((0, 256))
-        quantise_act((256, 256))
-        product(2, WIDE, scale_on_scalar)
-        quantise_wgt(0)
-        product(0, WIDE, scale_on_scalar)
-        weigh(3)
-        quantise_wgt(1)
-        product(1, WIDE, scale_on_scalar)
+
+        weigh(2)
         leaky(4)
-        quantise_wgt(3)
-        product(3, WIDE, scale_on_scalar)
+        quantise_act(HALVES[0])
+        quantise_wgt(2)
+        quantise_act(HALVES[1])
+        quantise_wgt(0)
         nc.vector.tensor_copy(out=act_by_neuron[:, block(4), :], in_=act_f32[:, block(4), :])
-        weigh(4)
+        quantise_wgt(1)
+        weigh(3)
+        for b in (2, 0, 1):
+            for part in HALVES:
+                product(b, part, scale_on_scalar)
         quantise_act(NARROW)
         narrow_01 = multiply_narrow(0)
-        narrow_23 = multiply_narrow(2)
-        quantise_wgt(4)
-        last = [multiply(4, part) for part in ((0, 256), (256, 256), (512, 128))]
+        quantise_wgt(3)
+        weigh(4)
         store_narrow(0, narrow_01, scale_on_vector)
-        store_narrow(2, narrow_23, scale_on_scalar)
-        store(4, (0, 256), last[0], scale_on_vector)
-        store(4, (256, 256), last[1], scale_on_scalar)
-        store(4, (512, 128), last[2], scale_on_vector)
+        for part in HALVES:
+            product(3, part, scale_on_scalar)
+        store_narrow(2, multiply_narrow(2), scale_on_scalar)
+        quantise_wgt(4)
+        last = [multiply(4, part) for part in HALVES + (NARROW,)]
+        store(4, HALVES[0], last[0], scale_on_vector)
+        store(4, HALVES[1], last[1], scale_on_scalar)
+        store(4, NARROW, last[2], scale_on_vector)

@@ -18,6 +18,7 @@ NEURONS = 640
 BLOCK = 128
 N_BLOCKS = NEURONS // BLOCK
 HALVES = ((0, 256), (256, 256))
+WIDE = (0, 512)
 NARROW = (512, 128)
 SLOPE = 0.01
 SAMPLE_PAIRS = (slice(0, 2), slice(2, 4))
@@ -31,7 +32,7 @@ def tile_mnelayer_pb_s_kernel(tc, potential, contribution, out):
     nc = tc.nc
     with ExitStack() as ctx:
         keep = ctx.enter_context(tc.tile_pool(name="keep", bufs=1))
-        stored = ctx.enter_context(tc.tile_pool(name="stored", bufs=14))
+        stored = ctx.enter_context(tc.tile_pool(name="stored", bufs=10))
         psum = ctx.enter_context(tc.psum_pool(name="psum", bufs=7))
         idle = ctx.enter_context(tc.psum_pool(name="idle", bufs=1))
 
@@ -151,7 +152,7 @@ def tile_mnelayer_pb_s_kernel(tc, potential, contribution, out):
 
         ctx.enter_context(tc.manual_schedule())
 
-        nc.scalar.dma_start(out=contrib[:], in_=contribution.rearrange("(p t) -> p t", t=PACK))
+        nc.sync.dma_start(out=contrib[:], in_=contribution.rearrange("(p t) -> p t", t=PACK))
         by_partition = potential.rearrange("(p t) w -> p t w", t=PACK)
 
         def load(samples, neurons):
@@ -213,16 +214,16 @@ def tile_mnelayer_pb_s_kernel(tc, potential, contribution, out):
         nc.vector.tensor_copy(out=act_by_neuron[:, block(4), :], in_=act_f32[:, block(4), :])
         quantise_wgt(1)
         weigh(3)
-        for b in (2, 0, 1):
-            for part in HALVES:
-                product(b, part, scale_on_scalar)
+        for part in HALVES:
+            product(2, part, scale_on_scalar)
+        for b in (0, 1):
+            product(b, WIDE, scale_on_scalar)
         quantise_act(NARROW)
         narrow_01 = multiply_narrow(0)
         quantise_wgt(3)
         weigh(4)
         store_narrow(0, narrow_01, scale_on_vector)
-        for part in HALVES:
-            product(3, part, scale_on_scalar)
+        product(3, WIDE, scale_on_scalar)
         store_narrow(2, multiply_narrow(2), scale_on_scalar)
         quantise_wgt(4)
         last = [multiply(4, part) for part in HALVES + (NARROW,)]

@@ -20,6 +20,7 @@ N_BLOCKS = NEURONS // BLOCK
 HALVES = ((0, 256), (256, 256))
 WIDE = (0, 512)
 NARROW = (512, 128)
+RUN = 4
 SLOPE = 0.01
 SAMPLE_PAIRS = (slice(0, 2), slice(2, 4))
 ON_TENSOR = 2
@@ -41,8 +42,7 @@ def tile_mnelayer_pb_s_kernel(tc, potential, contribution, out):
         contrib_f32 = keep.tile([P, PACK], F32)
         ident = keep.tile([P, P], F32)
         diag = keep.tile([P, PACK, P], F32)
-        act_rows = keep.tile([P, PACK, ON_TENSOR * BLOCK], F32)
-        act_f32 = keep.tile([P, NEURONS, PACK], F32)
+        act_rows = keep.tile([P, PACK, NEURONS], F32)
         act_by_neuron = keep.tile([P, NEURONS, PACK], BF16, align_bytes=64)
         wgt_by_neuron = keep.tile([P, NEURONS, PACK], BF16, align_bytes=64)
         act_codes = keep.tile([P, NEURONS], U32, align_bytes=64)
@@ -69,31 +69,26 @@ def tile_mnelayer_pb_s_kernel(tc, potential, contribution, out):
         def quantise_wgt(b):
             quantise(wgt_by_neuron, wgt_codes, wgt_scales, block(b))
 
-        def leaky(b):
-            x = pot[:, :, block(b)].rearrange("p t w -> p w t")
+        def by_runs(rows):
+            return rows.rearrange("p t (c i) -> p c t i", i=RUN)
+
+        def by_neuron(words):
+            return words.rearrange("p (c i) t -> p c t i", i=RUN)
+
+        def leaky(b, samples=slice(0, PACK)):
+            x = pot[:, samples, block(b)]
             nc.vector.scalar_tensor_tensor(
-                out=act_f32[:, block(b), :], in0=x, scalar=SLOPE, in1=x, op0=ALU.mult, op1=ALU.max
+                out=act_rows[:, samples, block(b)], in0=x, scalar=SLOPE, in1=x, op0=ALU.mult, op1=ALU.max
             )
 
-        def cast(b):
-            nc.scalar.copy(out=act_by_neuron[:, block(b), :], in_=act_f32[:, block(b), :])
-
-        def activate_rows(b):
-            for pair in SAMPLE_PAIRS:
-                x = pot[:, pair, block(b)]
-                nc.vector.scalar_tensor_tensor(
-                    out=act_rows[:, pair, block(b)], in0=x, scalar=SLOPE, in1=x, op0=ALU.mult, op1=ALU.max
-                )
-            nc.scalar.copy(
-                out=act_by_neuron[:, block(b), :],
-                in_=act_rows[:, :, block(b)].rearrange("p t w -> p w t"),
-            )
+        def cast(b, copy):
+            copy(out=by_neuron(act_by_neuron[:, block(b), :]), in_=by_runs(act_rows[:, :, block(b)]))
 
         def weigh(b):
             nc.vector.tensor_tensor(
-                out=wgt_by_neuron[:, block(b), :],
-                in0=act_f32[:, block(b), :],
-                in1=contrib[:].unsqueeze(1).to_broadcast([P, BLOCK, PACK]),
+                out=by_neuron(wgt_by_neuron[:, block(b), :]),
+                in0=by_runs(act_rows[:, :, block(b)]),
+                in1=contrib[:].unsqueeze(1).unsqueeze(3).to_broadcast([P, BLOCK // RUN, PACK, RUN]),
                 op=ALU.mult,
             )
 
@@ -119,9 +114,11 @@ def tile_mnelayer_pb_s_kernel(tc, potential, contribution, out):
                 stop=True,
             )
 
-        def multiply(b, part):
-            bank = psum.tile([P, part[1]], F32)
-            pass_mx(bank[:], b, part)
+        def multiply(b, *parts):
+            bank = psum.tile([P, sum(part[1] for part in parts)], F32)
+            for part in parts:
+                start = part[0] - parts[0][0]
+                pass_mx(bank[:, start : start + part[1]], b, part)
             return bank
 
         def multiply_narrow(first):
@@ -197,11 +194,13 @@ def tile_mnelayer_pb_s_kernel(tc, potential, contribution, out):
 
         banks = []
         for b in range(ON_TENSOR):
-            activate_rows(b)
+            for pair in SAMPLE_PAIRS:
+                leaky(b, pair)
+            cast(b, nc.scalar.copy)
             banks.append(weigh_on_tensor(b))
         for b in (2, 3):
             leaky(b)
-            cast(b)
+            cast(b, nc.scalar.copy)
         for b in range(ON_TENSOR):
             round_weighed(b, banks[b])
 
@@ -211,7 +210,7 @@ def tile_mnelayer_pb_s_kernel(tc, potential, contribution, out):
         quantise_wgt(2)
         quantise_act(HALVES[1])
         quantise_wgt(0)
-        nc.vector.tensor_copy(out=act_by_neuron[:, block(4), :], in_=act_f32[:, block(4), :])
+        cast(4, nc.vector.tensor_copy)
         quantise_wgt(1)
         weigh(3)
         for part in HALVES:
@@ -224,9 +223,8 @@ def tile_mnelayer_pb_s_kernel(tc, potential, contribution, out):
         weigh(4)
         store_narrow(0, narrow_01, scale_on_vector)
         product(3, WIDE, scale_on_scalar)
-        store_narrow(2, multiply_narrow(2), scale_on_scalar)
+        narrow_23 = multiply_narrow(2)
         quantise_wgt(4)
-        last = [multiply(4, part) for part in HALVES + (NARROW,)]
-        store(4, HALVES[0], last[0], scale_on_vector)
-        store(4, HALVES[1], last[1], scale_on_scalar)
-        store(4, NARROW, last[2], scale_on_vector)
+        store_narrow(2, narrow_23, scale_on_vector)
+        store(4, (0, 384), multiply(4, (0, 256), (256, 128)), scale_on_vector)
+        store(4, (384, 256), multiply(4, (384, 256)), scale_on_scalar)

@@ -121,10 +121,10 @@ def tile_mnelayer_pb_s_kernel(tc, potential, contribution, out):
                 pass_mx(bank[:, start : start + part[1]], b, part)
             return bank
 
-        def multiply_narrow(first):
-            bank = psum.tile([P, 2, BLOCK], F32)
-            for i in range(2):
-                pass_mx(bank[:, i, :], first + i, NARROW)
+        def multiply_narrow(count):
+            bank = psum.tile([P, count, BLOCK], F32)
+            for b in range(count):
+                pass_mx(bank[:, b, :], b, NARROW)
             return bank
 
         def scale_on_scalar(dst, src):
@@ -138,10 +138,10 @@ def tile_mnelayer_pb_s_kernel(tc, potential, contribution, out):
             scale(piece[:], bank[:])
             nc.sync.dma_start(out=out[block(b), columns(part)], in_=piece[:])
 
-        def store_narrow(first, bank, scale):
-            piece = stored.tile([P, 2, BLOCK], F32)
+        def store_narrow(count, bank, scale):
+            piece = stored.tile([P, count, BLOCK], F32)
             scale(piece[:], bank[:])
-            rows = out[first * BLOCK : (first + 2) * BLOCK, columns(NARROW)]
+            rows = out[: count * BLOCK, columns(NARROW)]
             nc.sync.dma_start(out=rows.rearrange("(i p) c -> p i c", p=P), in_=piece[:])
 
         def product(b, part, scale):
@@ -218,13 +218,18 @@ def tile_mnelayer_pb_s_kernel(tc, potential, contribution, out):
         for b in (0, 1):
             product(b, WIDE, scale_on_scalar)
         quantise_act(NARROW)
-        narrow_01 = multiply_narrow(0)
+        narrow_012 = multiply_narrow(3)
         quantise_wgt(3)
         weigh(4)
-        store_narrow(0, narrow_01, scale_on_vector)
-        product(3, WIDE, scale_on_scalar)
-        narrow_23 = multiply_narrow(2)
+        store_narrow(3, narrow_012, scale_on_scalar)
+        row_3 = stored.tile([P, NEURONS], F32)
+        wide_3, narrow_3 = multiply(3, WIDE), multiply(3, NARROW)
+        scale_on_scalar(row_3[:, columns(WIDE)], wide_3[:])
         quantise_wgt(4)
-        store_narrow(2, narrow_23, scale_on_vector)
-        store(4, (0, 384), multiply(4, (0, 256), (256, 128)), scale_on_vector)
-        store(4, (384, 256), multiply(4, (384, 256)), scale_on_scalar)
+        scale_on_vector(row_3[:, columns(NARROW)], narrow_3[:])
+        nc.sync.dma_start(out=out[block(3), :], in_=row_3[:])
+        row_4 = stored.tile([P, NEURONS], F32)
+        left_4, right_4 = multiply(4, (0, 256), (256, 128)), multiply(4, (384, 256))
+        scale_on_vector(row_4[:, 0:384], left_4[:])
+        scale_on_scalar(row_4[:, 384:640], right_4[:])
+        nc.sync.dma_start(out=out[block(4), :], in_=row_4[:])

@@ -160,12 +160,11 @@ def tile_mnelayer_pb_s_kernel(tc, potential, contribution, out):
         load(slice(0, PACK), slice(256, 512))
         load(slice(0, PACK), slice(512, 640))
 
-        make_identity(nc, ident[:])
-
         zeros = keep.tile([P, PACK * BLOCK], BF16, align_bytes=64)
         zero_codes = keep.tile([P, BLOCK], U32, align_bytes=64)
         zero_scales = keep.tile([P, BLOCK], U8, align_bytes=64)
-        nc.vector.memset(zeros[:].bitcast(I32), 0)
+        nc.gpsimd.memset(zeros[:].bitcast(I32), 0)
+        make_identity(nc, ident[:])
         nc.vector.quantize_mx(out=zero_codes[:].bitcast(FP8X4), scales=zero_scales[:], in_=zeros[:])
         unread = idle.tile([P, BLOCK], F32)
 
@@ -205,9 +204,9 @@ def tile_mnelayer_pb_s_kernel(tc, potential, contribution, out):
             round_weighed(b, banks[b])
 
         weigh(2)
-        leaky(4)
         quantise_act(HALVES[0])
         quantise_wgt(2)
+        leaky(4)
         quantise_act(HALVES[1])
         quantise_wgt(0)
         cast(4, nc.vector.tensor_copy)

@@ -101,7 +101,7 @@ def tile_mnelayer_pb_s_kernel(tc, potential, contribution, out):
             return bank
 
         def round_weighed(b, bank):
-            nc.scalar.copy(out=wgt_by_neuron[:, block(b), :], in_=bank[:].rearrange("p t w -> p w t"))
+            nc.scalar.copy(out=by_neuron(wgt_by_neuron[:, block(b), :]), in_=by_runs(bank[:]))
 
         def pass_mx(dst, b, part):
             nc.tensor.matmul_mx(

from contextlib import ExitStack

import concourse.mybir as mybir
from concourse.masks import make_identity

F32 = mybir.dt.float32
BF16 = mybir.dt.bfloat16
U32 = mybir.dt.uint32
U8 = mybir.dt.uint8
I32 = mybir.dt.int32
FP8X4 = mybir.dt.float8_e4m3fn_x4
ALU = mybir.AluOpType

P = 128
PACK = 4
SAMPLES = P * PACK
NEURONS = 640
BLOCK = 128
N_BLOCKS = NEURONS // BLOCK
HALVES = ((0, 256), (256, 256))
WIDE = (0, 512)
NARROW = (512, 128)
RUN = 4
SLOPE = 0.01
SAMPLE_PAIRS = (slice(0, 2), slice(2, 4))
ON_TENSOR = 2
WARM_PASSES = 16

FLOPS = 2 * SAMPLES * NEURONS * NEURONS


def tile_mnelayer_pb_s_kernel(tc, potential, contribution, out):
    nc = tc.nc
    with ExitStack() as ctx:
        keep = ctx.enter_context(tc.tile_pool(name="keep", bufs=1))
        stored = ctx.enter_context(tc.tile_pool(name="stored", bufs=10))
        psum = ctx.enter_context(tc.psum_pool(name="psum", bufs=7))
        idle = ctx.enter_context(tc.psum_pool(name="idle", bufs=1))

        pot = keep.tile([P, PACK, NEURONS], BF16)
        contrib = keep.tile([P, PACK], BF16)
        contrib_f32 = keep.tile([P, PACK], F32)
        ident = keep.tile([P, P], F32)
        diag = keep.tile([P, PACK, P], F32)
        act_rows = keep.tile([P, PACK, NEURONS], F32)
        act_by_neuron = keep.tile([P, NEURONS, PACK], BF16, align_bytes=64)
        wgt_by_neuron = keep.tile([P, NEURONS, PACK], BF16, align_bytes=64)
        act_codes = keep.tile([P, NEURONS], U32, align_bytes=64)
        act_scales = keep.tile([P, NEURONS], U8, align_bytes=64)
        wgt_codes = keep.tile([P, NEURONS], U32, align_bytes=64)
        wgt_scales = keep.tile([P, NEURONS], U8, align_bytes=64)

        def block(b):
            return slice(b * BLOCK, (b + 1) * BLOCK)

        def columns(part):
            return slice(part[0], part[0] + part[1])

        def quantise(values, codes, scales, neurons):
            nc.vector.quantize_mx(
                out=codes[:, neurons].bitcast(FP8X4),
                scales=scales[:, neurons],
                in_=values[:, neurons, :].rearrange("p w t -> p (w t)"),
            )

        def quantise_act(part):
            quantise(act_by_neuron, act_codes, act_scales, columns(part))

        def quantise_wgt(b):
            quantise(wgt_by_neuron, wgt_codes, wgt_scales, block(b))

        def by_runs(rows):
            return rows.rearrange("p t (c i) -> p c t i", i=RUN)

        def by_neuron(words):
            return words.rearrange("p (c i) t -> p c t i", i=RUN)

        def leaky(b, samples=slice(0, PACK)):
            x = pot[:, samples, block(b)]
            nc.vector.scalar_tensor_tensor(
                out=act_rows[:, samples, block(b)], in0=x, scalar=SLOPE, in1=x, op0=ALU.mult, op1=ALU.max
            )

        def cast(b, copy):
            copy(out=by_neuron(act_by_neuron[:, block(b), :]), in_=by_runs(act_rows[:, :, block(b)]))

        def weigh(b):
            nc.vector.tensor_tensor(
                out=by_neuron(wgt_by_neuron[:, block(b), :]),
                in0=by_runs(act_rows[:, :, block(b)]),
                in1=contrib[:].unsqueeze(1).unsqueeze(3).to_broadcast([P, BLOCK // RUN, PACK, RUN]),
                op=ALU.mult,
            )

        def weigh_on_tensor(b):
            bank = psum.tile([P, PACK, BLOCK], F32)
            for t in range(PACK):
                nc.tensor.matmul(
                    out=bank[:, t, :], lhsT=diag[:, t, :], rhs=act_rows[:, t, block(b)], start=True, stop=True
                )
            return bank

        def round_weighed(b, bank):
            nc.scalar.copy(out=by_neuron(wgt_by_neuron[:, block(b), :]), in_=by_runs(bank[:]))

        def pass_mx(dst, b, part):
            nc.tensor.matmul_mx(
                out=dst,
                lhsT=wgt_codes[:, block(b)].bitcast(FP8X4),
                lhsT_scale=wgt_scales[:, block(b)],
                rhs=act_codes[:, columns(part)].bitcast(FP8X4),
                rhs_scale=act_scales[:, columns(part)],
                start=True,
                stop=True,
            )

        def multiply(b, *parts):
            bank = psum.tile([P, sum(part[1] for part in parts)], F32)
            for part in parts:
                start = part[0] - parts[0][0]
                pass_mx(bank[:, start : start + part[1]], b, part)
            return bank

        def multiply_narrow(count):
            bank = psum.tile([P, count, BLOCK], F32)
            for b in range(count):
                pass_mx(bank[:, b, :], b, NARROW)
            return bank

        def scale_on_scalar(dst, src):
            nc.scalar.mul(out=dst, in_=src, mul=1.0 / SAMPLES)

        def scale_on_vector(dst, src):
            nc.vector.tensor_scalar_mul(out=dst, in0=src, scalar1=1.0 / SAMPLES)

        def store(b, part, bank, scale):
            piece = stored.tile([P, part[1]], F32)
            scale(piece[:], bank[:])
            nc.sync.dma_start(out=out[block(b), columns(part)], in_=piece[:])

        def store_narrow(count, bank, scale):
            piece = stored.tile([P, count, BLOCK], F32)
            scale(piece[:], bank[:])
            rows = out[: count * BLOCK, columns(NARROW)]
            nc.sync.dma_start(out=rows.rearrange("(i p) c -> p i c", p=P), in_=piece[:])

        def product(b, part, scale):
            store(b, part, multiply(b, part), scale)

        ctx.enter_context(tc.manual_schedule())

        nc.sync.dma_start(out=contrib[:], in_=contribution.rearrange("(p t) -> p t", t=PACK))
        by_partition = potential.rearrange("(p t) w -> p t w", t=PACK)

        def load(samples, neurons):
            nc.sync.dma_start(out=pot[:, samples, neurons], in_=by_partition[:, samples, neurons])

        for pair in SAMPLE_PAIRS:
            load(pair, slice(0, 256))
        load(slice(0, PACK), slice(256, 512))
        load(slice(0, PACK), slice(512, 640))

        zeros = keep.tile([P, PACK * BLOCK], BF16, align_bytes=64)
        zero_codes = keep.tile([P, BLOCK], U32, align_bytes=64)
        zero_scales = keep.tile([P, BLOCK], U8, align_bytes=64)
        nc.gpsimd.memset(zeros[:].bitcast(I32), 0)
        make_identity(nc, ident[:])
        nc.vector.quantize_mx(out=zero_codes[:].bitcast(FP8X4), scales=zero_scales[:], in_=zeros[:])
        unread = idle.tile([P, BLOCK], F32)

        def idle_passes(count):
            for i in range(count):
                nc.tensor.matmul_mx(
                    out=unread[:],
                    lhsT=zero_codes[:].bitcast(FP8X4),
                    lhsT_scale=zero_scales[:],
                    rhs=zero_codes[:].bitcast(FP8X4),
                    rhs_scale=zero_scales[:],
                    start=True,
                    stop=True,
                )

        idle_passes(WARM_PASSES)

        nc.scalar.copy(out=contrib_f32[:], in_=contrib[:])
        for t in range(PACK):
            nc.scalar.activation(
                out=diag[:, t, :],
                in_=ident[:],
                func=mybir.ActivationFunctionType.Copy,
                scale=contrib_f32[:, t : t + 1],
            )

        banks = []
        for b in range(ON_TENSOR):
            for pair in SAMPLE_PAIRS:
                leaky(b, pair)
            cast(b, nc.scalar.copy)
            banks.append(weigh_on_tensor(b))
        for b in (2, 3):
            leaky(b)
            cast(b, nc.scalar.copy)
        for b in range(ON_TENSOR):
            round_weighed(b, banks[b])

        weigh(2)
        quantise_act(HALVES[0])
        quantise_wgt(2)
        leaky(4)
        quantise_act(HALVES[1])
        quantise_wgt(0)
        cast(4, nc.vector.tensor_copy)
        quantise_wgt(1)
        weigh(3)
        for part in HALVES:
            product(2, part, scale_on_scalar)
        for b in (0, 1):
            product(b, WIDE, scale_on_scalar)
        quantise_act(NARROW)
        narrow_012 = multiply_narrow(3)
        quantise_wgt(3)
        weigh(4)
        store_narrow(3, narrow_012, scale_on_scalar)
        row_3 = stored.tile([P, NEURONS], F32)
        wide_3, narrow_3 = multiply(3, WIDE), multiply(3, NARROW)
        scale_on_scalar(row_3[:, columns(WIDE)], wide_3[:])
        quantise_wgt(4)
        scale_on_vector(row_3[:, columns(NARROW)], narrow_3[:])
        nc.sync.dma_start(out=out[block(3), :], in_=row_3[:])
        row_4 = stored.tile([P, NEURONS], F32)
        left_4, right_4 = multiply(4, (0, 256), (256, 128)), multiply(4, (384, 256))
        scale_on_vector(row_4[:, 0:384], left_4[:])
        scale_on_scalar(row_4[:, 384:640], right_4[:])
        nc.sync.dma_start(out=out[block(4), :], in_=row_4[:])
